import numpy as np
import ml_dtypes

BF16 = ml_dtypes.bfloat16


def bf(x):
    return np.asarray(x, np.float32).astype(BF16)


def f32(x):
    return np.asarray(x, np.float32)


def f64(x):
    return np.asarray(x).astype(np.float64)


def striped(idx):
    return np.tile(idx.reshape(-1, 16).T, (8, 1))


K, C, S, M, N = 4, 1024, 256, 256, 1024


def setup_inputs():
    return {"x": f32(np.random.standard_normal((K, C, S))), "offs": striped(np.concatenate([np.random.permutation(S) for _ in range(-(-(N) // S))])[:N])}


def reference(x, offs):
    idx = offs[:16].T.reshape(-1)
    x = f64(x)
    acc = np.zeros((C, M))
    for q in range(K):
        acc = acc + x[q][:, idx[q * M:(q + 1) * M]]
    return acc

@@ -1,0 +1,42 @@
+import concourse.mybir as mybir
+
+F32 = mybir.dt.float32
+U16 = mybir.dt.uint16
+ADD = mybir.AluOpType.add
+
+P = 128
+CELLS = 4
+POSITIONS = 1024
+CHANNELS = 256
+BLOCKS = POSITIONS // P
+PIECE_COLS = CHANNELS // 16
+
+
+def tile_convproduct_kernel(tc, x, offs, out):
+    nc = tc.nc
+    with (
+        tc.tile_pool(name="held", bufs=1) as held,
+        tc.tile_pool(name="windows", bufs=CELLS * BLOCKS) as windows,
+        tc.tile_pool(name="sums", bufs=2 * CELLS) as sums,
+    ):
+        offsets = held.tile([P, CELLS * PIECE_COLS], U16, name="offsets")
+        nc.sync.dma_start(offsets[:], offs)
+
+        window = {}
+        for b in range(BLOCKS):
+            for q in range(CELLS):
+                window[b, q] = windows.tile([P, CHANNELS], F32, name="window")
+                nc.sync.dma_start(window[b, q][:], x[q, b * P : (b + 1) * P, :])
+
+        for b in range(BLOCKS):
+            before = None
+            for q in range(CELLS):
+                piece = offsets[:, q * PIECE_COLS : (q + 1) * PIECE_COLS]
+                picked = window[b, q][:].indirect(piece)
+                total = sums.tile([P, CHANNELS], F32, name="total")
+                if q == 0:
+                    nc.vector.tensor_copy(total[:], picked)
+                else:
+                    nc.vector.tensor_tensor(total[:], picked, before[:], ADD)
+                before = total
+            nc.sync.dma_start(out[b * P : (b + 1) * P, :], total[:])

@@ -10,6 +10,7 @@ POSITIONS = 1024
 CHANNELS = 256
 BLOCKS = POSITIONS // P
 PIECE_COLS = CHANNELS // 16
+TOGETHER = 2
 
 
 def tile_convproduct_kernel(tc, x, offs, out):
@@ -17,26 +18,32 @@ def tile_convproduct_kernel(tc, x, offs, out):
     with (
         tc.tile_pool(name="held", bufs=1) as held,
         tc.tile_pool(name="windows", bufs=CELLS * BLOCKS) as windows,
-        tc.tile_pool(name="sums", bufs=2 * CELLS) as sums,
+        tc.tile_pool(name="sums", bufs=2 * CELLS * TOGETHER) as sums,
     ):
         offsets = held.tile([P, CELLS * PIECE_COLS], U16, name="offsets")
         nc.sync.dma_start(offsets[:], offs)
 
-        window = {}
-        for b in range(BLOCKS):
-            for q in range(CELLS):
-                window[b, q] = windows.tile([P, CHANNELS], F32, name="window")
-                nc.sync.dma_start(window[b, q][:], x[q, b * P : (b + 1) * P, :])
+        order = [
+            (b, q)
+            for first in range(0, BLOCKS, TOGETHER)
+            for q in range(CELLS)
+            for b in range(first, first + TOGETHER)
+        ]
 
-        for b in range(BLOCKS):
-            before = None
-            for q in range(CELLS):
-                piece = offsets[:, q * PIECE_COLS : (q + 1) * PIECE_COLS]
-                picked = window[b, q][:].indirect(piece)
-                total = sums.tile([P, CHANNELS], F32, name="total")
-                if q == 0:
-                    nc.vector.tensor_copy(total[:], picked)
-                else:
-                    nc.vector.tensor_tensor(total[:], picked, before[:], ADD)
-                before = total
-            nc.sync.dma_start(out[b * P : (b + 1) * P, :], total[:])
+        window = {}
+        for b, q in order:
+            window[b, q] = windows.tile([P, CHANNELS], F32, name="window")
+            nc.sync.dma_start(window[b, q][:], x[q, b * P : (b + 1) * P, :])
+
+        total = {}
+        for b, q in order:
+            piece = offsets[:, q * PIECE_COLS : (q + 1) * PIECE_COLS]
+            picked = window[b, q][:].indirect(piece)
+            longer = sums.tile([P, CHANNELS], F32, name="longer")
+            if q == 0:
+                nc.vector.tensor_copy(longer[:], picked)
+            else:
+                nc.vector.tensor_tensor(longer[:], picked, total[b][:], ADD)
+            total[b] = longer
+            if q == CELLS - 1:
+                nc.sync.dma_start(out[b * P : (b + 1) * P, :], total[b][:])

@@ -31,9 +31,10 @@ def tile_convproduct_kernel(tc, x, offs, out):
         ]
 
         window = {}
-        for b, q in order:
+        for i, (b, q) in enumerate(order):
             window[b, q] = windows.tile([P, CHANNELS], F32, name="window")
-            nc.sync.dma_start(window[b, q][:], x[q, b * P : (b + 1) * P, :])
+            queue = nc.scalar if i % 2 == 0 else nc.sync
+            queue.dma_start(window[b, q][:], x[q, b * P : (b + 1) * P, :])
 
         total = {}
         for b, q in order:

@@ -10,7 +10,6 @@ POSITIONS = 1024
 CHANNELS = 256
 BLOCKS = POSITIONS // P
 PIECE_COLS = CHANNELS // 16
-TOGETHER = 2
 
 
 def tile_convproduct_kernel(tc, x, offs, out):
@@ -18,33 +17,29 @@ def tile_convproduct_kernel(tc, x, offs, out):
     with (
         tc.tile_pool(name="held", bufs=1) as held,
         tc.tile_pool(name="windows", bufs=CELLS * BLOCKS) as windows,
-        tc.tile_pool(name="sums", bufs=2 * CELLS * TOGETHER) as sums,
+        tc.tile_pool(name="sums", bufs=2 * BLOCKS) as sums,
     ):
         offsets = held.tile([P, CELLS * PIECE_COLS], U16, name="offsets")
         nc.sync.dma_start(offsets[:], offs)
 
-        order = [
-            (b, q)
-            for first in range(0, BLOCKS, TOGETHER)
-            for q in range(CELLS)
-            for b in range(first, first + TOGETHER)
-        ]
-
         window = {}
-        for i, (b, q) in enumerate(order):
-            window[b, q] = windows.tile([P, CHANNELS], F32, name="window")
-            queue = nc.scalar if i % 2 == 0 else nc.sync
-            queue.dma_start(window[b, q][:], x[q, b * P : (b + 1) * P, :])
+        for q in range(CELLS):
+            for b in range(BLOCKS):
+                window[q, b] = windows.tile([P, CHANNELS], F32, name="window")
+                queue = nc.scalar if b % 2 == 0 else nc.sync
+                queue.dma_start(window[q, b][:], x[q, b * P : (b + 1) * P, :])
 
         total = {}
-        for b, q in order:
+        for q in range(CELLS):
             piece = offsets[:, q * PIECE_COLS : (q + 1) * PIECE_COLS]
-            picked = window[b, q][:].indirect(piece)
-            longer = sums.tile([P, CHANNELS], F32, name="longer")
-            if q == 0:
-                nc.vector.tensor_copy(longer[:], picked)
-            else:
-                nc.vector.tensor_tensor(longer[:], picked, total[b][:], ADD)
-            total[b] = longer
-            if q == CELLS - 1:
-                nc.sync.dma_start(out[b * P : (b + 1) * P, :], total[b][:])
+            for b in range(BLOCKS):
+                picked = window[q, b][:].indirect(piece)
+                longer = sums.tile([P, CHANNELS], F32, name="longer")
+                if q == 0:
+                    nc.vector.tensor_copy(longer[:], picked)
+                else:
+                    nc.vector.tensor_tensor(longer[:], picked, total[b][:], ADD)
+                total[b] = longer
+
+        for b in range(BLOCKS):
+            nc.sync.dma_start(out[b * P : (b + 1) * P, :], total[b][:])

@@ -10,6 +10,7 @@ POSITIONS = 1024
 CHANNELS = 256
 BLOCKS = POSITIONS // P
 PIECE_COLS = CHANNELS // 16
+SIDE_BY_SIDE = 2
 
 
 def tile_convproduct_kernel(tc, x, offs, out):
@@ -23,23 +24,28 @@ def tile_convproduct_kernel(tc, x, offs, out):
         nc.sync.dma_start(offsets[:], offs)
 
         window = {}
-        for q in range(CELLS):
-            for b in range(BLOCKS):
-                window[q, b] = windows.tile([P, CHANNELS], F32, name="window")
-                queue = nc.scalar if b % 2 == 0 else nc.sync
-                queue.dma_start(window[q, b][:], x[q, b * P : (b + 1) * P, :])
+        for pair in range(0, BLOCKS, SIDE_BY_SIDE):
+            for q in range(CELLS):
+                for b in range(pair, pair + SIDE_BY_SIDE):
+                    window[q, b] = windows.tile([P, CHANNELS], F32, name="window")
+                    queue = nc.scalar if b % 2 == 0 else nc.sync
+                    queue.dma_start(window[q, b][:], x[q, b * P : (b + 1) * P, :])
 
         total = {}
-        for q in range(CELLS):
-            piece = offsets[:, q * PIECE_COLS : (q + 1) * PIECE_COLS]
-            for b in range(BLOCKS):
-                picked = window[q, b][:].indirect(piece)
-                longer = sums.tile([P, CHANNELS], F32, name="longer")
-                if q == 0:
-                    nc.vector.tensor_copy(longer[:], picked)
-                else:
-                    nc.vector.tensor_tensor(longer[:], picked, total[b][:], ADD)
-                total[b] = longer
-
-        for b in range(BLOCKS):
-            nc.sync.dma_start(out[b * P : (b + 1) * P, :], total[b][:])
+        for pair in range(0, BLOCKS, SIDE_BY_SIDE):
+            for q in range(CELLS):
+                for b in range(pair, pair + SIDE_BY_SIDE):
+                    longer = sums.tile([P, CHANNELS], F32, name="longer")
+                    parts = 2 if (q, b) == (CELLS - 1, BLOCKS - 1) else 1
+                    width = CHANNELS // parts
+                    for h in range(parts):
+                        columns = slice(h * width, (h + 1) * width)
+                        first = q * PIECE_COLS + h * width // 16
+                        picked = window[q, b][:].indirect(offsets[:, first : first + width // 16])
+                        if q == 0:
+                            nc.vector.tensor_copy(longer[:, columns], picked)
+                        else:
+                            nc.vector.tensor_tensor(longer[:, columns], picked, total[b][:, columns], ADD)
+                        if q == CELLS - 1:
+                            nc.sync.dma_start(out[b * P : (b + 1) * P, columns], longer[:, columns])
+                    total[b] = longer

@@ -11,6 +11,7 @@ CHANNELS = 256
 BLOCKS = POSITIONS // P
 PIECE_COLS = CHANNELS // 16
 SIDE_BY_SIDE = 2
+WARM = 64
 
 
 def tile_convproduct_kernel(tc, x, offs, out):
@@ -30,6 +31,13 @@ def tile_convproduct_kernel(tc, x, offs, out):
                     window[q, b] = windows.tile([P, CHANNELS], F32, name="window")
                     queue = nc.scalar if b % 2 == 0 else nc.sync
                     queue.dma_start(window[q, b][:], x[q, b * P : (b + 1) * P, :])
+
+        zeros = held.tile([P, WARM], F32, name="zeros")
+        copied = held.tile([P, WARM], F32, name="copied")
+        added = held.tile([P, WARM], F32, name="added")
+        nc.vector.memset(zeros[:], 0.0)
+        nc.vector.tensor_copy(copied[:], zeros[:])
+        nc.vector.tensor_tensor(added[:], zeros[:], copied[:], ADD)
 
         total = {}
         for pair in range(0, BLOCKS, SIDE_BY_SIDE):

import concourse.mybir as mybir

F32 = mybir.dt.float32
U16 = mybir.dt.uint16
ADD = mybir.AluOpType.add

P = 128
CELLS = 4
POSITIONS = 1024
CHANNELS = 256
BLOCKS = POSITIONS // P
PIECE_COLS = CHANNELS // 16
SIDE_BY_SIDE = 2
WARM = 64


def tile_convproduct_kernel(tc, x, offs, out):
    nc = tc.nc
    with (
        tc.tile_pool(name="held", bufs=1) as held,
        tc.tile_pool(name="windows", bufs=CELLS * BLOCKS) as windows,
        tc.tile_pool(name="sums", bufs=2 * BLOCKS) as sums,
    ):
        offsets = held.tile([P, CELLS * PIECE_COLS], U16, name="offsets")
        nc.sync.dma_start(offsets[:], offs)

        window = {}
        for pair in range(0, BLOCKS, SIDE_BY_SIDE):
            for q in range(CELLS):
                for b in range(pair, pair + SIDE_BY_SIDE):
                    window[q, b] = windows.tile([P, CHANNELS], F32, name="window")
                    queue = nc.scalar if b % 2 == 0 else nc.sync
                    queue.dma_start(window[q, b][:], x[q, b * P : (b + 1) * P, :])

        zeros = held.tile([P, WARM], F32, name="zeros")
        copied = held.tile([P, WARM], F32, name="copied")
        added = held.tile([P, WARM], F32, name="added")
        nc.vector.memset(zeros[:], 0.0)
        nc.vector.tensor_copy(copied[:], zeros[:])
        nc.vector.tensor_tensor(added[:], zeros[:], copied[:], ADD)

        total = {}
        for pair in range(0, BLOCKS, SIDE_BY_SIDE):
            for q in range(CELLS):
                for b in range(pair, pair + SIDE_BY_SIDE):
                    longer = sums.tile([P, CHANNELS], F32, name="longer")
                    parts = 2 if (q, b) == (CELLS - 1, BLOCKS - 1) else 1
                    width = CHANNELS // parts
                    for h in range(parts):
                        columns = slice(h * width, (h + 1) * width)
                        first = q * PIECE_COLS + h * width // 16
                        picked = window[q, b][:].indirect(offsets[:, first : first + width // 16])
                        if q == 0:
                            nc.vector.tensor_copy(longer[:, columns], picked)
                        else:
                            nc.vector.tensor_tensor(longer[:, columns], picked, total[b][:, columns], ADD)
                        if q == CELLS - 1:
                            nc.sync.dma_start(out[b * P : (b + 1) * P, columns], longer[:, columns])
                    total[b] = longer
